import numpy as np
import ml_dtypes


def mxq(x, axis, fmt="e4m3"):
    dtype, down = {"e4m3": (ml_dtypes.float8_e4m3fn, 7), "e5m2": (ml_dtypes.float8_e5m2, 14)}[fmt]
    v = np.moveaxis(np.asarray(x, np.float32).astype(ml_dtypes.bfloat16).astype(np.float64), axis, -1)
    blocks = v.reshape(v.shape[:-1] + (-1, 32))
    amax = np.abs(blocks).max(-1, keepdims=True)
    byte = np.maximum(np.where(amax > 0, np.frexp(amax)[1] - 1 + 127, 0) - down, 1)
    scale = np.exp2(byte - 127.0)
    codes = (blocks / scale).astype(np.float32).astype(dtype).astype(np.float64)
    return np.moveaxis((codes * scale).reshape(v.shape), -1, axis)


WIDE = False


def mx_kscale(k):
    if not WIDE:
        return np.ones(k)
    levels = np.array([10, -10, 5, -5, 0])
    if k % 512:
        return np.exp2(np.random.permutation(np.resize(levels, k // 32))).repeat(32)
    a = np.empty((k // 512, 16))
    for p in range(k // 512):
        a[p, :8] = np.random.permutation(np.resize(levels, 8))
        for g in range(8):
            far = levels[np.abs(levels - a[p, g]) >= 10]
            a[p, g + 8] = far[np.random.randint(len(far))]
    return np.exp2(a.ravel()).repeat(32)


BF16 = ml_dtypes.bfloat16


def bf(x):
    return np.asarray(x, np.float32).astype(BF16)


def f64(x):
    return np.asarray(x).astype(np.float64)


B, T, C, H, KH, D = 4, 128, 2048, 16, 4, 128
HALF = D // 2
RMS_EPS = 1e-6


def rms_norm(v, w):
    var = np.mean(v * v, axis=-1, keepdims=True)
    return v * (1.0 / np.sqrt(var + RMS_EPS)) * w


def rotary(v, cos, sin):
    v1, v2 = v[..., :HALF], v[..., HALF:]
    return np.concatenate([v1 * cos - v2 * sin, v1 * sin + v2 * cos], axis=-1)


def draw0():
    s = mx_kscale(C)
    return {"x": bf(np.random.standard_normal((B, T, C)) * s),
            "cos": bf(np.random.uniform(0.0, 1.0, (1, T, 1, HALF))),
            "sin": bf(np.random.uniform(0.0, 1.0, (1, T, 1, HALF))),
            "wq": bf(np.random.standard_normal((C, H * D)) / np.sqrt(C) / s[:, None]),
            "wk": bf(np.random.standard_normal((C, KH * D)) / np.sqrt(C) / s[:, None]),
            "q_norm_w": bf(1.0 + 0.1 * np.random.standard_normal(D)),
            "k_norm_w": bf(1.0 + 0.1 * np.random.standard_normal(D))}


def core(x, cos, sin, wq, wk, q_norm_w, k_norm_w):
    xq = mxq(f64(x), 2, "e4m3")
    q = (xq @ mxq(f64(wq), 0, "e4m3")).reshape(B, T, H, D)
    k = (xq @ mxq(f64(wk), 0, "e4m3")).reshape(B, T, KH, D)
    q = rms_norm(q, f64(q_norm_w))
    k = rms_norm(k, f64(k_norm_w))
    q = rotary(q, f64(cos), f64(sin))
    k = rotary(k, f64(cos), f64(sin))
    return q, k


def e4m3fn_bytes(y):
    return np.clip(np.asarray(y, np.float64), -448.0, 448.0).astype(np.float32).astype(ml_dtypes.float8_e4m3fn).view(np.uint8)


def e4m3fn_values(b):
    return np.asarray(b, np.uint8).view(ml_dtypes.float8_e4m3fn).astype(np.float64)


def setup_inputs():
    d = draw0()
    x0 = np.asarray(d['wq']).astype(np.float64)
    s = (np.max(np.abs(x0), axis=(1,), keepdims=True) / 448.0).astype(np.float32)
    out = {}
    for k, v in d.items():
        if k == 'wq':
            out['wq_bytes'] = e4m3fn_bytes(x0 / s.astype(np.float64))
            out['wq_scale'] = s
        else:
            out[k] = v
    return out


def reference(x, cos, sin, wq_bytes, wq_scale, wk, q_norm_w, k_norm_w):
    return core(x, cos, sin, e4m3fn_values(wq_bytes) * wq_scale.astype(np.float64), wk, q_norm_w, k_norm_w)

@@ -1,0 +1,303 @@
+from contextlib import ExitStack
+
+import concourse.mybir as mybir
+from concourse.masks import make_identity
+
+F32 = mybir.dt.float32
+BF16 = mybir.dt.bfloat16
+U32 = mybir.dt.uint32
+U8 = mybir.dt.uint8
+FP8 = mybir.dt.float8_e4m3fn
+FP8X4 = mybir.dt.float8_e4m3fn_x4
+ACT = mybir.ActivationFunctionType
+ALU = mybir.AluOpType
+
+NB, T, C, H, KH, D = 4, 128, 2048, 16, 4, 128
+HALF = D // 2
+EPS = 1e-6
+P = 128
+PASSES = C // 512
+NCH = 5
+FLOPS = 2 * NB * T * C * (H + KH) * D
+S_UNITS = ()
+RUN = 8
+
+
+def tile_multiheadattention_pa_kernel(
+    tc, x, cos, sin, wq_bytes, wq_scale, wk, q_norm_w, k_norm_w, out_0, out_1
+):
+    nc = tc.nc
+    with ExitStack() as ctx:
+        const = ctx.enter_context(tc.tile_pool(name="const", bufs=1))
+        keep = ctx.enter_context(tc.tile_pool(name="keep", bufs=1))
+        w16p = ctx.enter_context(tc.tile_pool(name="w16p", bufs=6))
+        wgp = ctx.enter_context(tc.tile_pool(name="wgp", bufs=4))
+        epi = ctx.enter_context(tc.tile_pool(name="epi", bufs=4))
+        small = ctx.enter_context(tc.tile_pool(name="small", bufs=8))
+        psum = ctx.enter_context(tc.psum_pool(name="psum", bufs=8))
+        ctx.enter_context(tc.manual_schedule())
+
+        one1 = const.tile([P, 1], F32, name="one1")
+        nc.vector.memset(one1[:], 1.0)
+        warm = const.tile([P, 1], F32, name="warm")
+        nc.scalar.activation(out=warm[:], in_=one1[:], func=ACT.Abs_reciprocal_sqrt)
+        sc = const.tile([P, 4 * PASSES], F32, name="sc")
+        nc.sync.dma_start(
+            out=sc[:].rearrange("p (g t) -> p g t", t=4),
+            in_=wq_scale.rearrange("(g p t) o -> p g (t o)", p=P, t=4),
+        )
+        grow = const.tile([P, 2 * D], BF16, name="grow")
+        nc.vector.memset(grow[:].bitcast(F32), 0.0)
+        nc.gpsimd.dma_start(out=grow[0:1, 0:D], in_=q_norm_w.unsqueeze(0))
+        nc.gpsimd.dma_start(out=grow[0:1, D : 2 * D], in_=k_norm_w.unsqueeze(0))
+        cs = const.tile([P, 2 * HALF], BF16, name="cs")
+        nc.gpsimd.dma_start(out=cs[:, 0:HALF], in_=cos.rearrange("o t u d -> (o t) (u d)"))
+        nc.gpsimd.dma_start(out=cs[:, HALF : 2 * HALF], in_=sin.rearrange("o t u d -> (o t) (u d)"))
+        ones = const.tile([P, P], BF16, name="ones")
+        nc.vector.memset(ones[:], 1.0)
+        ident = const.tile([P, P], F32, name="ident")
+        make_identity(nc, ident[:])
+
+        wq_v = wq_bytes.rearrange("(g p t) n -> g p t n", p=P, t=4)
+        wk_v = wk.rearrange("(g p t) n -> g p t n", p=P, t=4)
+        xin = [keep.tile([P, C], BF16, name="xin%d" % b) for b in range(NB)]
+        wkin = [keep.tile([P, 4, 512], BF16, name="wkin%d" % g) for g in range(1, PASSES)]
+        wkin0 = [keep.tile([P, 4, 256], BF16, name="wkin0_%d" % hf) for hf in range(2)]
+        wqb = [
+            [keep.tile([P, 4, 512], U8, name="wqb%d_%d" % (j, g)) for g in range(PASSES)]
+            for j in range(4)
+        ]
+
+        def load_wq(j, g):
+            nc.sync.dma_start(out=wqb[j][g][:], in_=wq_v[g][:, :, 512 * j : 512 * (j + 1)])
+
+        for hf in range(2):
+            nc.sync.dma_start(out=wqb[0][0][:, 2 * hf : 2 * hf + 2, :], in_=wq_v[0][:, 2 * hf : 2 * hf + 2, 0:512])
+        for hf in range(2):
+            nc.sync.dma_start(out=wkin0[hf][:], in_=wk_v[0][:, :, 256 * hf : 256 * (hf + 1)])
+        for g in range(1, PASSES):
+            load_wq(0, g)
+            nc.sync.dma_start(out=wkin[g - 1][:], in_=wk_v[g])
+        for b in range(NB):
+            nc.sync.dma_start(out=xin[b][:], in_=x[b])
+        for j in range(1, 4):
+            for g in range(PASSES):
+                load_wq(j, g)
+
+        tabq = const.tile([P, 2 * D], F32, name="tabq")
+        tabk = const.tile([P, 2 * D], F32, name="tabk")
+
+        gains = []
+
+        def spread_gains():
+            gps = psum.tile([P, 512], F32, tag="bank", name="gps")
+            nc.tensor.matmul(out=gps[:, 0 : 2 * D], lhsT=ones[:], rhs=grow[:], start=True, stop=True)
+            gains.append(gps)
+
+        def tables():
+            gps = gains[0]
+            for i, tab in enumerate((tabq, tabk)):
+                g1 = gps[:, i * D : i * D + HALF]
+                g2 = gps[:, i * D + HALF : (i + 1) * D]
+                cc = cs[:, 0:HALF]
+                ssn = cs[:, HALF : 2 * HALF]
+                nc.vector.tensor_tensor(out=tab[:, 0:HALF], in0=g1, in1=cc, op=ALU.mult)
+                nc.vector.scalar_tensor_tensor(
+                    out=tab[:, HALF:D], in0=g2, scalar=-1.0, in1=ssn, op0=ALU.mult, op1=ALU.mult
+                )
+                nc.vector.tensor_tensor(out=tab[:, D : D + HALF], in0=g1, in1=ssn, op=ALU.mult)
+                nc.vector.tensor_tensor(out=tab[:, D + HALF : 2 * D], in0=g2, in1=cc, op=ALU.mult)
+
+        xc = [keep.tile([P, 512], U32, name="xc%d" % b, align_bytes=64) for b in range(NB)]
+        xs = [keep.tile([P, 512], U8, name="xs%d" % b, align_bytes=64) for b in range(NB)]
+        xg = [keep.tile([P, C], BF16, name="xg%d" % b, align_bytes=64) for b in range(NB)]
+        wc = [keep.tile([P, PASSES * 512], U32, name="wc%d" % c, align_bytes=64) for c in range(NCH)]
+        ws = [keep.tile([P, PASSES * 512], U8, name="ws%d" % c, align_bytes=64) for c in range(NCH)]
+        w16 = {}
+        wg = {}
+        acc = {}
+        rr = {}
+        abt = {}
+
+        def x_turn(b):
+            words = xin[b][:].bitcast(F32)
+            xgw = xg[b][:].bitcast(F32)
+            for hf in range(2):
+                bank = psum.tile([P, 512], F32, tag="bank", name="xt%d_%d" % (b, hf))
+                for gi in range(2):
+                    g = 2 * hf + gi
+                    for u in range(2):
+                        nc.tensor.transpose(
+                            bank[:, (2 * gi + u) * P : (2 * gi + u + 1) * P],
+                            words[:, 256 * g + u : 256 * (g + 1) : 2],
+                            ident[:],
+                        )
+                nc.scalar.copy(
+                    out=xgw[:, 512 * hf : 512 * (hf + 1)].rearrange("p (g r u) -> p g r u", g=2, u=2),
+                    in_=bank[:].rearrange("p (g u r) -> p g r u", g=2, u=2),
+                )
+
+        def x_quant(b):
+            nc.vector.quantize_mx(out=xc[b][:].bitcast(FP8X4), scales=xs[b][:], in_=xg[b][:])
+
+        def widen(c, g):
+            t16 = w16p.tile([P, 4, 512], BF16, tag="w16", name="w16_%d_%d" % (c, g))
+            for t in range(4):
+                nc.scalar.activation(
+                    out=t16[:, t, :],
+                    in_=wqb[c - 1][g][:, t, :].bitcast(FP8),
+                    func=ACT.Copy,
+                    scale=sc[:, 4 * g + t : 4 * g + t + 1],
+                )
+            w16[(c, g)] = t16
+            if (c, g) in S_UNITS:
+                tg = wgp.tile([P, 2048], BF16, tag="wgs", name="wgs_%d_%d" % (c, g), align_bytes=64, bufs=1)
+                nc.scalar.copy(
+                    out=tg[:].rearrange("p (n t) -> p n t", t=4), in_=t16[:].rearrange("p t n -> p n t")
+                )
+                wg[(c, g)] = tg
+
+        def interleave(c, g):
+            if (c, g) in S_UNITS:
+                return
+            srcs = wkin0 if (c, g) == (0, 0) else [wkin[g - 1]] if c == 0 else [w16[(c, g)]]
+            tg = wgp.tile([P, 2048], BF16, tag="wg", name="wg_%d_%d" % (c, g), align_bytes=64)
+            w = 2048 // len(srcs)
+            for q, src in enumerate(srcs):
+                nc.vector.tensor_copy(
+                    out=tg[:, w * q : w * (q + 1)].rearrange("p (c i t) -> p c t i", i=RUN, t=4),
+                    in_=src[:].rearrange("p t (c i) -> p c t i", i=RUN),
+                )
+            wg[(c, g)] = tg
+
+        def quantize(c, g):
+            cols = slice(512 * g, 512 * (g + 1))
+            nc.vector.quantize_mx(out=wc[c][:, cols].bitcast(FP8X4), scales=ws[c][:, cols], in_=wg[(c, g)][:])
+
+        def matmul(c, g, b):
+            if g == 0:
+                acc[(c, b)] = psum.tile([P, 512], F32, tag="bank", name="acc%d_%d" % (c, b))
+            cols = slice(512 * g, 512 * (g + 1))
+            nc.tensor.matmul_mx(
+                out=acc[(c, b)][:],
+                lhsT=xc[b][:, P * g : P * (g + 1)].bitcast(FP8X4),
+                lhsT_scale=xs[b][:, P * g : P * (g + 1)],
+                rhs=wc[c][:, cols].bitcast(FP8X4),
+                rhs_scale=ws[c][:, cols],
+                start=(g == 0),
+                stop=(g == PASSES - 1),
+            )
+
+        def squares(c, b0):
+            ss = small.tile([P, 8], F32, tag="ss", name="ss_%d_%d" % (c, b0))
+            r = small.tile([P, 8], F32, tag="r", name="r_%d_%d" % (c, b0))
+            for i in range(8):
+                a = acc[(c, b0 + i // 4)]
+                h = i % 4
+                junk = small.tile([P, D], BF16, tag="junk", name="junk_%d_%d_%d" % (c, b0, i))
+                nc.scalar.activation(
+                    out=junk[:], in_=a[:, h * D : (h + 1) * D], func=ACT.Square, accum_out=ss[:, i : i + 1]
+                )
+            nc.scalar.activation(out=r[:], in_=ss[:], func=ACT.Abs_reciprocal_sqrt, scale=1.0 / D, bias=EPS)
+            rr[(c, b0)] = r[:, 0:4]
+            rr[(c, b0 + 1)] = r[:, 4:8]
+
+        def products(c, b, heads):
+            a = acc[(c, b)]
+            tab = tabk if c == 0 else tabq
+            if heads[0] == 0:
+                abt[(c, b)] = epi.tile([P, 4, 2, D], F32, tag="ab", name="ab_%d_%d" % (c, b))
+            ab = abt[(c, b)]
+            for h in heads:
+                nc.vector.scalar_tensor_tensor(
+                    out=ab[:, h, :, :],
+                    in0=a[:, h * D : (h + 1) * D].unsqueeze(1).to_broadcast([P, 2, D]),
+                    scalar=rr[(c, b)][:, h : h + 1],
+                    in1=tab[:].rearrange("p (u d) -> p u d", u=2),
+                    op0=ALU.mult,
+                    op1=ALU.mult,
+                )
+
+        def add_store(c, b, eng):
+            ab = abt[(c, b)]
+            o = epi.tile([P, 4, D], F32, tag="o", name="o_%d_%d" % (c, b))
+            pairs = ab[:].rearrange("p h u (e j) -> p (h u) e j", e=2)
+            eng.tensor_tensor(
+                out=o[:].rearrange("p h (u j) -> p (h u) j", u=2), in0=pairs[:, :, 0, :], in1=pairs[:, :, 1, :], op=ALU.add
+            )
+            if c == 0:
+                nc.sync.dma_start(out=out_1[b], in_=o[:])
+            else:
+                nc.sync.dma_start(out=out_0[b][:, 4 * (c - 1) : 4 * c, :], in_=o[:])
+
+        carried = []
+
+        def finish_carried():
+            for c, b in carried:
+                products(c, b, (3,))
+                add_store(c, b, nc.gpsimd)
+            carried.clear()
+
+        def epilogue(c):
+            for b in range(2):
+                products(c, b, (0, 1, 2, 3))
+                add_store(c, b, nc.gpsimd)
+            products(c, 2, (0, 1, 2, 3))
+            if c < NCH - 1:
+                products(c, NB - 1, (0, 1, 2))
+                add_store(c, 2, nc.vector)
+                carried.append((c, NB - 1))
+            else:
+                products(c, NB - 1, (0, 1, 2, 3))
+                add_store(c, 2, nc.vector)
+                add_store(c, 3, nc.vector)
+
+        units = [(c, g) for c in range(NCH) for g in range(PASSES)]
+        for g in range(PASSES):
+            widen(1, g)
+        for i in range(len(units) + 1):
+            if i == 5:
+                for b in range(NB):
+                    x_turn(b)
+                spread_gains()
+            if i == 7:
+                tables()
+            if i < len(units):
+                interleave(*units[i])
+            if i >= 1:
+                quantize(*units[i - 1])
+                if units[i - 1][0] >= 1 and i >= 8:
+                    for b in range(NB if units[i - 1][0] < 2 else NB - 1):
+                        matmul(units[i - 1][0], units[i - 1][1], b)
+            if i in (6, 7):
+                x_quant(2 * (i - 6))
+                x_quant(2 * (i - 6) + 1)
+            if i == 7:
+                for b in range(NB):
+                    for g in range(PASSES):
+                        matmul(0, g, b)
+                for g in range(3):
+                    for b in range(NB):
+                        matmul(1, g, b)
+                widen(2, 0)
+                squares(0, 0)
+                widen(2, 1)
+                squares(0, 2)
+                widen(2, 2)
+                widen(2, 3)
+            if i >= 8 and i % 4 == 0:
+                c = i // 4 - 1
+                if c + 2 < NCH:
+                    widen(c + 2, 0)
+                squares(c, 0)
+                finish_carried()
+                if c >= 2:
+                    for g in range(PASSES):
+                        matmul(c, g, NB - 1)
+                squares(c, 2)
+                if c + 2 < NCH:
+                    for g in range(1, PASSES):
+                        widen(c + 2, g)
+                epilogue(c - 1)
+        finish_carried()
+        epilogue(NCH - 1)

@@ -18,8 +18,8 @@ EPS = 1e-6
 P = 128
 PASSES = C // 512
 NCH = 5
+ORDER = [(0, 1, 3, 2), (0, 1, 2, 3)] + 3 * [(0, 1, 2, 3)]
 FLOPS = 2 * NB * T * C * (H + KH) * D
-S_UNITS = ()
 RUN = 8
 
 
@@ -30,17 +30,21 @@ def tile_multiheadattention_pa_kernel(
     with ExitStack() as ctx:
         const = ctx.enter_context(tc.tile_pool(name="const", bufs=1))
         keep = ctx.enter_context(tc.tile_pool(name="keep", bufs=1))
-        w16p = ctx.enter_context(tc.tile_pool(name="w16p", bufs=6))
+        w16p = ctx.enter_context(tc.tile_pool(name="w16p", bufs=5))
         wgp = ctx.enter_context(tc.tile_pool(name="wgp", bufs=4))
         epi = ctx.enter_context(tc.tile_pool(name="epi", bufs=4))
         small = ctx.enter_context(tc.tile_pool(name="small", bufs=8))
-        psum = ctx.enter_context(tc.psum_pool(name="psum", bufs=8))
+        psum = ctx.enter_context(tc.psum_pool(name="psum", bufs=6))
         ctx.enter_context(tc.manual_schedule())
 
         one1 = const.tile([P, 1], F32, name="one1")
         nc.vector.memset(one1[:], 1.0)
         warm = const.tile([P, 1], F32, name="warm")
         nc.scalar.activation(out=warm[:], in_=one1[:], func=ACT.Abs_reciprocal_sqrt)
+        ident = const.tile([P, P], F32, name="ident")
+        make_identity(nc, ident[:])
+        ident16 = const.tile([P, P], BF16, name="ident16")
+        nc.scalar.copy(out=ident16[:], in_=ident[:])
         sc = const.tile([P, 4 * PASSES], F32, name="sc")
         nc.sync.dma_start(
             out=sc[:].rearrange("p (g t) -> p g t", t=4),
@@ -55,14 +59,11 @@ def tile_multiheadattention_pa_kernel(
         nc.gpsimd.dma_start(out=cs[:, HALF : 2 * HALF], in_=sin.rearrange("o t u d -> (o t) (u d)"))
         ones = const.tile([P, P], BF16, name="ones")
         nc.vector.memset(ones[:], 1.0)
-        ident = const.tile([P, P], F32, name="ident")
-        make_identity(nc, ident[:])
 
         wq_v = wq_bytes.rearrange("(g p t) n -> g p t n", p=P, t=4)
         wk_v = wk.rearrange("(g p t) n -> g p t n", p=P, t=4)
         xin = [keep.tile([P, C], BF16, name="xin%d" % b) for b in range(NB)]
-        wkin = [keep.tile([P, 4, 512], BF16, name="wkin%d" % g) for g in range(1, PASSES)]
-        wkin0 = [keep.tile([P, 4, 256], BF16, name="wkin0_%d" % hf) for hf in range(2)]
+        wkin = [keep.tile([P, 4, 512], BF16, name="wkin%d" % g) for g in range(PASSES)]
         wqb = [
             [keep.tile([P, 4, 512], U8, name="wqb%d_%d" % (j, g)) for g in range(PASSES)]
             for j in range(4)
@@ -71,15 +72,25 @@ def tile_multiheadattention_pa_kernel(
         def load_wq(j, g):
             nc.sync.dma_start(out=wqb[j][g][:], in_=wq_v[g][:, :, 512 * j : 512 * (j + 1)])
 
+        def load_wk(g):
+            nc.sync.dma_start(out=wkin[g][:], in_=wk_v[g])
+
+        def load_x(b):
+            nc.sync.dma_start(out=xin[b][:], in_=x[b])
+
         for hf in range(2):
             nc.sync.dma_start(out=wqb[0][0][:, 2 * hf : 2 * hf + 2, :], in_=wq_v[0][:, 2 * hf : 2 * hf + 2, 0:512])
-        for hf in range(2):
-            nc.sync.dma_start(out=wkin0[hf][:], in_=wk_v[0][:, :, 256 * hf : 256 * (hf + 1)])
-        for g in range(1, PASSES):
-            load_wq(0, g)
-            nc.sync.dma_start(out=wkin[g - 1][:], in_=wk_v[g])
-        for b in range(NB):
-            nc.sync.dma_start(out=xin[b][:], in_=x[b])
+        load_wk(0)
+        load_wq(0, 1)
+        load_x(0)
+        load_wk(1)
+        load_wq(0, 2)
+        load_x(1)
+        load_wk(3)
+        load_x(2)
+        load_wk(2)
+        load_x(3)
+        load_wq(0, 3)
         for j in range(1, 4):
             for g in range(PASSES):
                 load_wq(j, g)
@@ -114,6 +125,7 @@ def tile_multiheadattention_pa_kernel(
         wc = [keep.tile([P, PASSES * 512], U32, name="wc%d" % c, align_bytes=64) for c in range(NCH)]
         ws = [keep.tile([P, PASSES * 512], U8, name="ws%d" % c, align_bytes=64) for c in range(NCH)]
         w16 = {}
+        turned = {}
         wg = {}
         acc = {}
         rr = {}
@@ -150,24 +162,47 @@ def tile_multiheadattention_pa_kernel(
                     scale=sc[:, 4 * g + t : 4 * g + t + 1],
                 )
             w16[(c, g)] = t16
-            if (c, g) in S_UNITS:
-                tg = wgp.tile([P, 2048], BF16, tag="wgs", name="wgs_%d_%d" % (c, g), align_bytes=64, bufs=1)
-                nc.scalar.copy(
-                    out=tg[:].rearrange("p (n t) -> p n t", t=4), in_=t16[:].rearrange("p t n -> p n t")
+
+        def widen_v(c, g):
+            t16 = w16p.tile([P, 4, 512], BF16, tag="w16v", name="w16_%d_%d" % (c, g), bufs=2)
+            for t in range(4):
+                nc.vector.tensor_scalar(
+                    out=t16[:, t, :],
+                    in0=wqb[c - 1][g][:, t, :].bitcast(FP8),
+                    scalar1=sc[:, 4 * g + t : 4 * g + t + 1],
+                    scalar2=None,
+                    op0=ALU.mult,
                 )
-                wg[(c, g)] = tg
+            w16[(c, g)] = t16
 
         def interleave(c, g):
-            if (c, g) in S_UNITS:
-                return
-            srcs = wkin0 if (c, g) == (0, 0) else [wkin[g - 1]] if c == 0 else [w16[(c, g)]]
+            src = wkin[g] if c == 0 else w16[(c, g)]
             tg = wgp.tile([P, 2048], BF16, tag="wg", name="wg_%d_%d" % (c, g), align_bytes=64)
-            w = 2048 // len(srcs)
-            for q, src in enumerate(srcs):
-                nc.vector.tensor_copy(
-                    out=tg[:, w * q : w * (q + 1)].rearrange("p (c i t) -> p c t i", i=RUN, t=4),
-                    in_=src[:].rearrange("p t (c i) -> p c t i", i=RUN),
-                )
+            nc.vector.tensor_copy(
+                out=tg[:].rearrange("p (c i t) -> p c t i", i=RUN, t=4),
+                in_=src[:].rearrange("p t (c i) -> p c t i", i=RUN),
+            )
+            wg[(c, g)] = tg
+
+        def turn(c, g):
+            src = wkin[g] if c == 0 else w16[(c, g)]
+            for hf in range(2):
+                bank = psum.tile([P, 1024], BF16, tag="turn", name="turn%d_%d_%d" % (c, g, hf), bufs=2)
+                turned[(c, g, hf)] = bank
+                for q in range(2):
+                    n0 = 256 * hf + 128 * q
+                    nc.tensor.matmul(
+                        out=bank[:, 512 * q : 512 * (q + 1)],
+                        lhsT=ident16[:],
+                        rhs=src[:, :, n0 : n0 + 128].rearrange("p t n -> p n t"),
+                        start=True,
+                        stop=True,
+                    )
+
+        def turned_copy(c, g):
+            tg = wgp.tile([P, 2048], BF16, tag="wgt", name="wgt_%d_%d" % (c, g), align_bytes=64)
+            for hf in range(2):
+                nc.scalar.copy(out=tg[:, 1024 * hf : 1024 * (hf + 1)], in_=turned[(c, g, hf)][:])
             wg[(c, g)] = tg
 
         def quantize(c, g):
@@ -175,7 +210,7 @@ def tile_multiheadattention_pa_kernel(
             nc.vector.quantize_mx(out=wc[c][:, cols].bitcast(FP8X4), scales=ws[c][:, cols], in_=wg[(c, g)][:])
 
         def matmul(c, g, b):
-            if g == 0:
+            if g == ORDER[c][0]:
                 acc[(c, b)] = psum.tile([P, 512], F32, tag="bank", name="acc%d_%d" % (c, b))
             cols = slice(512 * g, 512 * (g + 1))
             nc.tensor.matmul_mx(
@@ -184,8 +219,8 @@ def tile_multiheadattention_pa_kernel(
                 lhsT_scale=xs[b][:, P * g : P * (g + 1)],
                 rhs=wc[c][:, cols].bitcast(FP8X4),
                 rhs_scale=ws[c][:, cols],
-                start=(g == 0),
-                stop=(g == PASSES - 1),
+                start=(g == ORDER[c][0]),
+                stop=(g == ORDER[c][-1]),
             )
 
         def squares(c, b0):
@@ -252,52 +287,78 @@ def tile_multiheadattention_pa_kernel(
                 add_store(c, 2, nc.vector)
                 add_store(c, 3, nc.vector)
 
-        units = [(c, g) for c in range(NCH) for g in range(PASSES)]
-        for g in range(PASSES):
-            widen(1, g)
-        for i in range(len(units) + 1):
-            if i == 5:
-                for b in range(NB):
-                    x_turn(b)
-                spread_gains()
-            if i == 7:
-                tables()
-            if i < len(units):
-                interleave(*units[i])
-            if i >= 1:
-                quantize(*units[i - 1])
-                if units[i - 1][0] >= 1 and i >= 8:
-                    for b in range(NB if units[i - 1][0] < 2 else NB - 1):
-                        matmul(units[i - 1][0], units[i - 1][1], b)
-            if i in (6, 7):
-                x_quant(2 * (i - 6))
-                x_quant(2 * (i - 6) + 1)
-            if i == 7:
-                for b in range(NB):
-                    for g in range(PASSES):
-                        matmul(0, g, b)
-                for g in range(3):
-                    for b in range(NB):
-                        matmul(1, g, b)
-                widen(2, 0)
-                squares(0, 0)
-                widen(2, 1)
-                squares(0, 2)
-                widen(2, 2)
-                widen(2, 3)
-            if i >= 8 and i % 4 == 0:
-                c = i // 4 - 1
-                if c + 2 < NCH:
-                    widen(c + 2, 0)
-                squares(c, 0)
-                finish_carried()
-                if c >= 2:
-                    for g in range(PASSES):
-                        matmul(c, g, NB - 1)
-                squares(c, 2)
-                if c + 2 < NCH:
-                    for g in range(1, PASSES):
-                        widen(c + 2, g)
+        def passes(c, banks):
+            for b in banks:
+                for g in ORDER[c]:
+                    matmul(c, g, b)
+
+        def stage(c, late):
+            n = c + 2
+            finish_carried()
+            if c > 0:
                 epilogue(c - 1)
+            if n < NCH:
+                widen(n, 0)
+            passes(c, late)
+            if n < NCH:
+                turn(n, 0)
+            squares(c, 0)
+            squares(c, 2)
+            if n < NCH:
+                widen(n, 2)
+                turned_copy(n, 0)
+                widen(n, 1)
+
+        def turn_third(c):
+            if c < NCH:
+                turn(c, 2)
+                turned_copy(c, 2)
+
+        widen_v(1, 0)
+        widen(1, 1)
+        interleave(1, 0)
+        x_turn(0)
+        interleave(0, 0)
+        quantize(1, 0)
+        widen(1, 2)
+        interleave(0, 1)
+        quantize(0, 0)
+        x_turn(1)
+        x_quant(0)
+        turn(0, 3)
+        turned_copy(0, 3)
+        quantize(0, 1)
+        interleave(1, 1)
+        x_turn(2)
+        x_quant(1)
+        quantize(0, 3)
+        interleave(0, 2)
+        quantize(1, 1)
+        x_turn(3)
+        spread_gains()
+        x_quant(2)
+        quantize(0, 2)
+        widen(1, 3)
+        interleave(1, 2)
+        x_quant(3)
+        tables()
+        interleave(1, 3)
+        quantize(1, 2)
+        quantize(1, 3)
+        stage(0, range(NB))
+        passes(1, (0, 1))
+        turn_third(2)
+        stage(1, (2, 3))
+        for c in range(2, NCH):
+            quantize(c, 0)
+            matmul(c, 0, 0)
+            turn_third(c + 1)
+            widen_v(c, 3)
+            interleave(c, 1)
+            interleave(c, 3)
+            for g in (1, 2, 3):
+                quantize(c, g)
+                matmul(c, g, 0)
+            stage(c, (1, 2, 3))
         finish_carried()
         epilogue(NCH - 1)

@@ -18,7 +18,7 @@ EPS = 1e-6
 P = 128
 PASSES = C // 512
 NCH = 5
-ORDER = [(0, 1, 3, 2), (0, 1, 2, 3)] + 3 * [(0, 1, 2, 3)]
+V_WIDENS = ((1, 0), (2, 3))
 FLOPS = 2 * NB * T * C * (H + KH) * D
 RUN = 8
 
@@ -86,9 +86,9 @@ def tile_multiheadattention_pa_kernel(
         load_wk(1)
         load_wq(0, 2)
         load_x(1)
-        load_wk(3)
-        load_x(2)
         load_wk(2)
+        load_x(2)
+        load_wk(3)
         load_x(3)
         load_wq(0, 3)
         for j in range(1, 4):
@@ -210,7 +210,7 @@ def tile_multiheadattention_pa_kernel(
             nc.vector.quantize_mx(out=wc[c][:, cols].bitcast(FP8X4), scales=ws[c][:, cols], in_=wg[(c, g)][:])
 
         def matmul(c, g, b):
-            if g == ORDER[c][0]:
+            if g == 0:
                 acc[(c, b)] = psum.tile([P, 512], F32, tag="bank", name="acc%d_%d" % (c, b))
             cols = slice(512 * g, 512 * (g + 1))
             nc.tensor.matmul_mx(
@@ -219,8 +219,8 @@ def tile_multiheadattention_pa_kernel(
                 lhsT_scale=xs[b][:, P * g : P * (g + 1)],
                 rhs=wc[c][:, cols].bitcast(FP8X4),
                 rhs_scale=ws[c][:, cols],
-                start=(g == ORDER[c][0]),
-                stop=(g == ORDER[c][-1]),
+                start=(g == 0),
+                stop=(g == PASSES - 1),
             )
 
         def squares(c, b0):
@@ -289,7 +289,7 @@ def tile_multiheadattention_pa_kernel(
 
         def passes(c, banks):
             for b in banks:
-                for g in ORDER[c]:
+                for g in range(PASSES):
                     matmul(c, g, b)
 
         def stage(c, late):
@@ -305,14 +305,11 @@ def tile_multiheadattention_pa_kernel(
             squares(c, 0)
             squares(c, 2)
             if n < NCH:
-                widen(n, 2)
-                turned_copy(n, 0)
                 widen(n, 1)
-
-        def turn_third(c):
-            if c < NCH:
-                turn(c, 2)
-                turned_copy(c, 2)
+                turned_copy(n, 0)
+                for g in (2, 3):
+                    if (n, g) not in V_WIDENS:
+                        widen(n, g)
 
         widen_v(1, 0)
         widen(1, 1)
@@ -325,38 +322,38 @@ def tile_multiheadattention_pa_kernel(
         quantize(0, 0)
         x_turn(1)
         x_quant(0)
-        turn(0, 3)
-        turned_copy(0, 3)
         quantize(0, 1)
-        interleave(1, 1)
-        x_turn(2)
-        x_quant(1)
-        quantize(0, 3)
         interleave(0, 2)
-        quantize(1, 1)
+        x_quant(1)
+        x_turn(2)
+        interleave(0, 3)
+        quantize(0, 2)
+        x_quant(2)
         x_turn(3)
         spread_gains()
-        x_quant(2)
-        quantize(0, 2)
         widen(1, 3)
-        interleave(1, 2)
+        quantize(0, 3)
+        interleave(1, 1)
         x_quant(3)
         tables()
+        interleave(1, 2)
+        quantize(1, 1)
         interleave(1, 3)
         quantize(1, 2)
         quantize(1, 3)
         stage(0, range(NB))
-        passes(1, (0, 1))
-        turn_third(2)
-        stage(1, (2, 3))
+        stage(1, range(NB))
         for c in range(2, NCH):
             quantize(c, 0)
             matmul(c, 0, 0)
-            turn_third(c + 1)
-            widen_v(c, 3)
+            if (c, 3) in V_WIDENS:
+                widen_v(c, 3)
             interleave(c, 1)
+            interleave(c, 2)
+            quantize(c, 1)
+            matmul(c, 1, 0)
             interleave(c, 3)
-            for g in (1, 2, 3):
+            for g in (2, 3):
                 quantize(c, g)
                 matmul(c, g, 0)
             stage(c, (1, 2, 3))

@@ -18,7 +18,7 @@ EPS = 1e-6
 P = 128
 PASSES = C // 512
 NCH = 5
-V_WIDENS = ((1, 0), (2, 3))
+V_WIDENS = ((1, 0), (2, 3), (3, 3))
 FLOPS = 2 * NB * T * C * (H + KH) * D
 RUN = 8
 

@@ -18,6 +18,7 @@ EPS = 1e-6
 P = 128
 PASSES = C // 512
 NCH = 5
+ORDER = 2 * [(0, 1, 2, 3)] + 3 * [(1, 2, 0, 3)]
 V_WIDENS = ((1, 0), (2, 3), (3, 3))
 FLOPS = 2 * NB * T * C * (H + KH) * D
 RUN = 8
@@ -101,7 +102,7 @@ def tile_multiheadattention_pa_kernel(
         gains = []
 
         def spread_gains():
-            gps = psum.tile([P, 512], F32, tag="bank", name="gps")
+            gps = psum.tile([P, 512], F32, tag="bank", name="gps", bufs=6)
             nc.tensor.matmul(out=gps[:, 0 : 2 * D], lhsT=ones[:], rhs=grow[:], start=True, stop=True)
             gains.append(gps)
 
@@ -135,7 +136,7 @@ def tile_multiheadattention_pa_kernel(
             words = xin[b][:].bitcast(F32)
             xgw = xg[b][:].bitcast(F32)
             for hf in range(2):
-                bank = psum.tile([P, 512], F32, tag="bank", name="xt%d_%d" % (b, hf))
+                bank = psum.tile([P, 512], F32, tag="bank", name="xt%d_%d" % (b, hf), bufs=6)
                 for gi in range(2):
                     g = 2 * hf + gi
                     for u in range(2):
@@ -184,20 +185,17 @@ def tile_multiheadattention_pa_kernel(
             )
             wg[(c, g)] = tg
 
-        def turn(c, g):
-            src = wkin[g] if c == 0 else w16[(c, g)]
-            for hf in range(2):
-                bank = psum.tile([P, 1024], BF16, tag="turn", name="turn%d_%d_%d" % (c, g, hf), bufs=2)
-                turned[(c, g, hf)] = bank
-                for q in range(2):
-                    n0 = 256 * hf + 128 * q
-                    nc.tensor.matmul(
-                        out=bank[:, 512 * q : 512 * (q + 1)],
-                        lhsT=ident16[:],
-                        rhs=src[:, :, n0 : n0 + 128].rearrange("p t n -> p n t"),
-                        start=True,
-                        stop=True,
-                    )
+        def turn(c, g, quarters):
+            for q in quarters:
+                if q % 2 == 0:
+                    turned[(c, g, q // 2)] = psum.tile([P, 1024], BF16, tag="turn", name="turn%d_%d_%d" % (c, g, q), bufs=2)
+                nc.tensor.matmul(
+                    out=turned[(c, g, q // 2)][:, 512 * (q % 2) : 512 * (q % 2 + 1)],
+                    lhsT=ident16[:],
+                    rhs=w16[(c, g)][:, :, P * q : P * (q + 1)].rearrange("p t n -> p n t"),
+                    start=True,
+                    stop=True,
+                )
 
         def turned_copy(c, g):
             tg = wgp.tile([P, 2048], BF16, tag="wgt", name="wgt_%d_%d" % (c, g), align_bytes=64)
@@ -210,8 +208,11 @@ def tile_multiheadattention_pa_kernel(
             nc.vector.quantize_mx(out=wc[c][:, cols].bitcast(FP8X4), scales=ws[c][:, cols], in_=wg[(c, g)][:])
 
         def matmul(c, g, b):
-            if g == 0:
-                acc[(c, b)] = psum.tile([P, 512], F32, tag="bank", name="acc%d_%d" % (c, b))
+            if g == ORDER[c][0]:
+                last = c == NCH - 1 and b in (1, 2)
+                acc[(c, b)] = psum.tile(
+                    [P, 512], F32, tag="turn" if last else "bank", name="acc%d_%d" % (c, b), bufs=2 if last else 6
+                )
             cols = slice(512 * g, 512 * (g + 1))
             nc.tensor.matmul_mx(
                 out=acc[(c, b)][:],
@@ -219,8 +220,8 @@ def tile_multiheadattention_pa_kernel(
                 lhsT_scale=xs[b][:, P * g : P * (g + 1)],
                 rhs=wc[c][:, cols].bitcast(FP8X4),
                 rhs_scale=ws[c][:, cols],
-                start=(g == 0),
-                stop=(g == PASSES - 1),
+                start=(g == ORDER[c][0]),
+                stop=(g == ORDER[c][-1]),
             )
 
         def squares(c, b0):
@@ -289,7 +290,7 @@ def tile_multiheadattention_pa_kernel(
 
         def passes(c, banks):
             for b in banks:
-                for g in range(PASSES):
+                for g in ORDER[c]:
                     matmul(c, g, b)
 
         def stage(c, late):
@@ -300,16 +301,17 @@ def tile_multiheadattention_pa_kernel(
             if n < NCH:
                 widen(n, 0)
             passes(c, late)
-            if n < NCH:
-                turn(n, 0)
+            if n == 2:
+                turn(n, 0, range(4))
+            if 2 <= c < NCH - 1:
+                turned_copy(c + 1, 0)
             squares(c, 0)
             squares(c, 2)
-            if n < NCH:
-                widen(n, 1)
+            for g in range(1, PASSES):
+                if n < NCH and (n, g) not in V_WIDENS:
+                    widen(n, g)
+            if n == 2:
                 turned_copy(n, 0)
-                for g in (2, 3):
-                    if (n, g) not in V_WIDENS:
-                        widen(n, g)
 
         widen_v(1, 0)
         widen(1, 1)
@@ -344,18 +346,19 @@ def tile_multiheadattention_pa_kernel(
         stage(0, range(NB))
         stage(1, range(NB))
         for c in range(2, NCH):
-            quantize(c, 0)
-            matmul(c, 0, 0)
+            staged = (0,) if c + 1 < NCH else (0, 1, 2)
             if (c, 3) in V_WIDENS:
                 widen_v(c, 3)
             interleave(c, 1)
             interleave(c, 2)
-            quantize(c, 1)
-            matmul(c, 1, 0)
-            interleave(c, 3)
-            for g in (2, 3):
+            for i, g in enumerate(ORDER[c]):
                 quantize(c, g)
-                matmul(c, g, 0)
-            stage(c, (1, 2, 3))
+                for b in staged:
+                    matmul(c, g, b)
+                if c + 1 < NCH:
+                    turn(c + 1, 0, (i,))
+                if i == 0:
+                    interleave(c, 3)
+            stage(c, [b for b in range(NB) if b not in staged])
         finish_carried()
         epilogue(NCH - 1)

@@ -53,20 +53,16 @@ def tile_multiheadattention_pa_kernel(
         )
         grow = const.tile([P, 2 * D], BF16, name="grow")
         nc.vector.memset(grow[:].bitcast(F32), 0.0)
-        nc.gpsimd.dma_start(out=grow[0:1, 0:D], in_=q_norm_w.unsqueeze(0))
-        nc.gpsimd.dma_start(out=grow[0:1, D : 2 * D], in_=k_norm_w.unsqueeze(0))
         cs = const.tile([P, 2 * HALF], BF16, name="cs")
-        nc.gpsimd.dma_start(out=cs[:, 0:HALF], in_=cos.rearrange("o t u d -> (o t) (u d)"))
-        nc.gpsimd.dma_start(out=cs[:, HALF : 2 * HALF], in_=sin.rearrange("o t u d -> (o t) (u d)"))
         ones = const.tile([P, P], BF16, name="ones")
         nc.vector.memset(ones[:], 1.0)
 
         wq_v = wq_bytes.rearrange("(g p t) n -> g p t n", p=P, t=4)
         wk_v = wk.rearrange("(g p t) n -> g p t n", p=P, t=4)
-        xin = [keep.tile([P, C], BF16, name="xin%d" % b) for b in range(NB)]
-        wkin = [keep.tile([P, 4, 512], BF16, name="wkin%d" % g) for g in range(PASSES)]
+        xin = [keep.tile([P, C], BF16, name="xin%d" % b, align_bytes=256) for b in range(NB)]
+        wkin = [keep.tile([P, 4, 512], BF16, name="wkin%d" % g, align_bytes=256) for g in range(PASSES)]
         wqb = [
-            [keep.tile([P, 4, 512], U8, name="wqb%d_%d" % (j, g)) for g in range(PASSES)]
+            [keep.tile([P, 4, 512], U8, name="wqb%d_%d" % (j, g), align_bytes=256) for g in range(PASSES)]
             for j in range(4)
         ]
 
@@ -91,6 +87,10 @@ def tile_multiheadattention_pa_kernel(
         load_x(2)
         load_wk(3)
         load_x(3)
+        nc.sync.dma_start(out=grow[0:1, 0:D], in_=q_norm_w.unsqueeze(0))
+        nc.sync.dma_start(out=grow[0:1, D : 2 * D], in_=k_norm_w.unsqueeze(0))
+        nc.sync.dma_start(out=cs[:, 0:HALF], in_=cos.rearrange("o t u d -> (o t) (u d)"))
+        nc.sync.dma_start(out=cs[:, HALF : 2 * HALF], in_=sin.rearrange("o t u d -> (o t) (u d)"))
         load_wq(0, 3)
         for j in range(1, 4):
             for g in range(PASSES):
@@ -130,6 +130,7 @@ def tile_multiheadattention_pa_kernel(
         wg = {}
         acc = {}
         rr = {}
+        ssq = {}
         abt = {}
 
         def x_turn(b):
@@ -153,16 +154,16 @@ def tile_multiheadattention_pa_kernel(
         def x_quant(b):
             nc.vector.quantize_mx(out=xc[b][:].bitcast(FP8X4), scales=xs[b][:], in_=xg[b][:])
 
-        def widen(c, g):
-            t16 = w16p.tile([P, 4, 512], BF16, tag="w16", name="w16_%d_%d" % (c, g))
-            for t in range(4):
+        def widen(c, g, planes=range(4)):
+            if planes[0] == 0:
+                w16[(c, g)] = w16p.tile([P, 4, 512], BF16, tag="w16", name="w16_%d_%d" % (c, g))
+            for t in planes:
                 nc.scalar.activation(
-                    out=t16[:, t, :],
+                    out=w16[(c, g)][:, t, :],
                     in_=wqb[c - 1][g][:, t, :].bitcast(FP8),
                     func=ACT.Copy,
                     scale=sc[:, 4 * g + t : 4 * g + t + 1],
                 )
-            w16[(c, g)] = t16
 
         def widen_v(c, g):
             t16 = w16p.tile([P, 4, 512], BF16, tag="w16v", name="w16_%d_%d" % (c, g), bufs=2)
@@ -224,19 +225,28 @@ def tile_multiheadattention_pa_kernel(
                 stop=(g == ORDER[c][-1]),
             )
 
-        def squares(c, b0):
-            ss = small.tile([P, 8], F32, tag="ss", name="ss_%d_%d" % (c, b0))
-            r = small.tile([P, 8], F32, tag="r", name="r_%d_%d" % (c, b0))
-            for i in range(8):
-                a = acc[(c, b0 + i // 4)]
-                h = i % 4
-                junk = small.tile([P, D], BF16, tag="junk", name="junk_%d_%d_%d" % (c, b0, i))
+        def norm(c, half):
+            r = small.tile([P, 8], F32, tag="r", name="r_%d_%d" % (c, half))
+            nc.scalar.activation(
+                out=r[:], in_=ssq[(c, half)][:], func=ACT.Abs_reciprocal_sqrt, scale=1.0 / D, bias=EPS
+            )
+            for i in range(2):
+                rr[(c, 2 * half + i)] = r[:, 4 * i : 4 * i + 4]
+
+        def squares(c):
+            for i in range(16):
+                b, h = i // 4, i % 4
+                if i % 8 == 0:
+                    ssq[(c, i // 8)] = small.tile([P, 8], F32, tag="ss", name="ss_%d_%d" % (c, i // 8))
+                junk = small.tile([P, D], BF16, tag="junk", name="junk_%d_%d" % (c, i))
                 nc.scalar.activation(
-                    out=junk[:], in_=a[:, h * D : (h + 1) * D], func=ACT.Square, accum_out=ss[:, i : i + 1]
+                    out=junk[:],
+                    in_=acc[(c, b)][:, h * D : (h + 1) * D],
+                    func=ACT.Square,
+                    accum_out=ssq[(c, i // 8)][:, i % 8 : i % 8 + 1],
                 )
-            nc.scalar.activation(out=r[:], in_=ss[:], func=ACT.Abs_reciprocal_sqrt, scale=1.0 / D, bias=EPS)
-            rr[(c, b0)] = r[:, 0:4]
-            rr[(c, b0 + 1)] = r[:, 4:8]
+                if i == 8:
+                    norm(c, 0)
 
         def products(c, b, heads):
             a = acc[(c, b)]
@@ -254,17 +264,38 @@ def tile_multiheadattention_pa_kernel(
                     op1=ALU.mult,
                 )
 
-        def add_store(c, b, eng):
-            ab = abt[(c, b)]
-            o = epi.tile([P, 4, D], F32, tag="o", name="o_%d_%d" % (c, b))
-            pairs = ab[:].rearrange("p h u (e j) -> p (h u) e j", e=2)
+        sums = {}
+
+        def add(c, b, eng, h0=0, h1=4):
+            if h0 == 0:
+                sums[(c, b)] = epi.tile([P, 4, D], F32, tag="o", name="o_%d_%d" % (c, b))
+            pairs = abt[(c, b)][:, h0:h1, :, :].rearrange("p h u (e j) -> p (h u) e j", e=2)
             eng.tensor_tensor(
-                out=o[:].rearrange("p h (u j) -> p (h u) j", u=2), in0=pairs[:, :, 0, :], in1=pairs[:, :, 1, :], op=ALU.add
+                out=sums[(c, b)][:, h0:h1, :].rearrange("p h (u j) -> p (h u) j", u=2),
+                in0=pairs[:, :, 0, :],
+                in1=pairs[:, :, 1, :],
+                op=ALU.add,
             )
+
+        def store(c, b, h0=0, h1=4, queue=nc.sync):
+            src = sums[(c, b)][:, h0:h1, :]
             if c == 0:
-                nc.sync.dma_start(out=out_1[b], in_=o[:])
+                queue.dma_start(out=out_1[b][:, h0:h1, :], in_=src)
             else:
-                nc.sync.dma_start(out=out_0[b][:, 4 * (c - 1) : 4 * c, :], in_=o[:])
+                queue.dma_start(out=out_0[b][:, 4 * (c - 1) + h0 : 4 * (c - 1) + h1, :], in_=src)
+
+        def add_store(c, b, eng):
+            add(c, b, eng)
+            store(c, b)
+
+        def sum_on_tensor(c, b):
+            bank = psum.tile([P, 512], F32, tag="bank", name="sum_%d_%d" % (c, b), bufs=6)
+            pairs = abt[(c, b)][:].rearrange("p h u (e j) -> p (h u) e j", e=2)
+            for e in range(2):
+                nc.tensor.matmul(out=bank[:], lhsT=ident[:], rhs=pairs[:, :, e, :], start=(e == 0), stop=(e == 1))
+            sums[(c, b)] = epi.tile([P, 4, D], F32, tag="o", name="o_%d_%d" % (c, b))
+            nc.scalar.copy(out=sums[(c, b)][:].rearrange("p h d -> p (h d)"), in_=bank[:])
+            store(c, b, queue=nc.scalar)
 
         carried = []
 
@@ -279,14 +310,20 @@ def tile_multiheadattention_pa_kernel(
                 products(c, b, (0, 1, 2, 3))
                 add_store(c, b, nc.gpsimd)
             products(c, 2, (0, 1, 2, 3))
-            if c < NCH - 1:
-                products(c, NB - 1, (0, 1, 2))
-                add_store(c, 2, nc.vector)
-                carried.append((c, NB - 1))
-            else:
-                products(c, NB - 1, (0, 1, 2, 3))
-                add_store(c, 2, nc.vector)
-                add_store(c, 3, nc.vector)
+            products(c, NB - 1, (0, 1, 2))
+            add_store(c, 2, nc.vector)
+            carried.append((c, NB - 1))
+
+        def last_epilogue(c):
+            for b in range(2):
+                products(c, b, (0, 1, 2, 3))
+                add_store(c, b, nc.gpsimd)
+            products(c, 2, (0, 1, 2, 3))
+            products(c, 3, (0, 1, 2, 3))
+            add_store(c, 2, nc.vector)
+            for h in (0, 2):
+                add(c, 3, nc.vector, h, h + 2)
+                store(c, 3, h, h + 2)
 
         def passes(c, banks):
             for b in banks:
@@ -305,11 +342,15 @@ def tile_multiheadattention_pa_kernel(
                 turn(n, 0, range(4))
             if 2 <= c < NCH - 1:
                 turned_copy(c + 1, 0)
-            squares(c, 0)
-            squares(c, 2)
-            for g in range(1, PASSES):
-                if n < NCH and (n, g) not in V_WIDENS:
-                    widen(n, g)
+            squares(c)
+            if n < NCH:
+                widen(n, 1, (0,))
+            norm(c, 1)
+            if n < NCH:
+                widen(n, 1, (1, 2, 3))
+                for g in (2, 3):
+                    if (n, g) not in V_WIDENS:
+                        widen(n, g)
             if n == 2:
                 turned_copy(n, 0)
 
@@ -361,4 +402,4 @@ def tile_multiheadattention_pa_kernel(
                     interleave(c, 3)
             stage(c, [b for b in range(NB) if b not in staged])
         finish_carried()
-        epilogue(NCH - 1)
+        last_epilogue(NCH - 1)

@@ -59,10 +59,11 @@ def tile_multiheadattention_pa_kernel(
 
         wq_v = wq_bytes.rearrange("(g p t) n -> g p t n", p=P, t=4)
         wk_v = wk.rearrange("(g p t) n -> g p t n", p=P, t=4)
-        xin = [keep.tile([P, C], BF16, name="xin%d" % b, align_bytes=256) for b in range(NB)]
-        wkin = [keep.tile([P, 4, 512], BF16, name="wkin%d" % g, align_bytes=256) for g in range(PASSES)]
+        xin = [keep.tile([P, C], BF16, name="xin%d" % b) for b in range(NB)]
+        wkin = [None] + [keep.tile([P, 4, 512], BF16, name="wkin%d" % g) for g in range(1, PASSES)]
+        wkin0 = [keep.tile([P, 4, 256], BF16, name="wkin0_%d" % hf) for hf in range(2)]
         wqb = [
-            [keep.tile([P, 4, 512], U8, name="wqb%d_%d" % (j, g), align_bytes=256) for g in range(PASSES)]
+            [keep.tile([P, 4, 512], U8, name="wqb%d_%d" % (j, g)) for g in range(PASSES)]
             for j in range(4)
         ]
 
@@ -77,21 +78,23 @@ def tile_multiheadattention_pa_kernel(
 
         for hf in range(2):
             nc.sync.dma_start(out=wqb[0][0][:, 2 * hf : 2 * hf + 2, :], in_=wq_v[0][:, 2 * hf : 2 * hf + 2, 0:512])
-        load_wk(0)
+        for hf in range(2):
+            n0 = 256 * hf
+            nc.sync.dma_start(out=wkin0[hf][:], in_=wk_v[0][:, :, n0 : n0 + 256])
         load_wq(0, 1)
         load_x(0)
         load_wk(1)
-        load_wq(0, 2)
         load_x(1)
+        load_wq(0, 2)
         load_wk(2)
         load_x(2)
         load_wk(3)
         load_x(3)
+        load_wq(0, 3)
         nc.sync.dma_start(out=grow[0:1, 0:D], in_=q_norm_w.unsqueeze(0))
         nc.sync.dma_start(out=grow[0:1, D : 2 * D], in_=k_norm_w.unsqueeze(0))
         nc.sync.dma_start(out=cs[:, 0:HALF], in_=cos.rearrange("o t u d -> (o t) (u d)"))
         nc.sync.dma_start(out=cs[:, HALF : 2 * HALF], in_=sin.rearrange("o t u d -> (o t) (u d)"))
-        load_wq(0, 3)
         for j in range(1, 4):
             for g in range(PASSES):
                 load_wq(j, g)
@@ -154,37 +157,38 @@ def tile_multiheadattention_pa_kernel(
         def x_quant(b):
             nc.vector.quantize_mx(out=xc[b][:].bitcast(FP8X4), scales=xs[b][:], in_=xg[b][:])
 
+        def w16_tile(c, g, tag, bufs):
+            if (c, g) not in w16:
+                w16[(c, g)] = w16p.tile([P, 4, 512], BF16, tag=tag, name="w16_%d_%d" % (c, g), bufs=bufs)
+            return w16[(c, g)]
+
         def widen(c, g, planes=range(4)):
-            if planes[0] == 0:
-                w16[(c, g)] = w16p.tile([P, 4, 512], BF16, tag="w16", name="w16_%d_%d" % (c, g))
             for t in planes:
                 nc.scalar.activation(
-                    out=w16[(c, g)][:, t, :],
+                    out=w16_tile(c, g, "w16", 5)[:, t, :],
                     in_=wqb[c - 1][g][:, t, :].bitcast(FP8),
                     func=ACT.Copy,
                     scale=sc[:, 4 * g + t : 4 * g + t + 1],
                 )
 
-        def widen_v(c, g):
-            t16 = w16p.tile([P, 4, 512], BF16, tag="w16v", name="w16_%d_%d" % (c, g), bufs=2)
-            for t in range(4):
+        def widen_v(c, g, planes=range(4)):
+            for t in planes:
                 nc.vector.tensor_scalar(
-                    out=t16[:, t, :],
+                    out=w16_tile(c, g, "w16v", 2)[:, t, :],
                     in0=wqb[c - 1][g][:, t, :].bitcast(FP8),
                     scalar1=sc[:, 4 * g + t : 4 * g + t + 1],
                     scalar2=None,
                     op0=ALU.mult,
                 )
-            w16[(c, g)] = t16
 
-        def interleave(c, g):
-            src = wkin[g] if c == 0 else w16[(c, g)]
-            tg = wgp.tile([P, 2048], BF16, tag="wg", name="wg_%d_%d" % (c, g), align_bytes=64)
-            nc.vector.tensor_copy(
-                out=tg[:].rearrange("p (c i t) -> p c t i", i=RUN, t=4),
-                in_=src[:].rearrange("p t (c i) -> p c t i", i=RUN),
+        def interleave(c, g, n0=0, n1=512, copy=nc.vector.tensor_copy):
+            src = wkin0[n0 // 256][:] if (c, g) == (0, 0) else (wkin[g] if c == 0 else w16[(c, g)])[:, :, n0:n1]
+            if (c, g) not in wg:
+                wg[(c, g)] = wgp.tile([P, 2048], BF16, tag="wg", name="wg_%d_%d" % (c, g), align_bytes=64)
+            copy(
+                out=wg[(c, g)][:, 4 * n0 : 4 * n1].rearrange("p (c i t) -> p c t i", i=RUN, t=4),
+                in_=src.rearrange("p t (c i) -> p c t i", i=RUN),
             )
-            wg[(c, g)] = tg
 
         def turn(c, g, quarters):
             for q in quarters:
@@ -199,7 +203,7 @@ def tile_multiheadattention_pa_kernel(
                 )
 
         def turned_copy(c, g):
-            tg = wgp.tile([P, 2048], BF16, tag="wgt", name="wgt_%d_%d" % (c, g), align_bytes=64)
+            tg = wgp.tile([P, 2048], BF16, tag="wgt", name="wgt_%d_%d" % (c, g), align_bytes=64, bufs=2)
             for hf in range(2):
                 nc.scalar.copy(out=tg[:, 1024 * hf : 1024 * (hf + 1)], in_=turned[(c, g, hf)][:])
             wg[(c, g)] = tg
@@ -265,10 +269,11 @@ def tile_multiheadattention_pa_kernel(
                 )
 
         sums = {}
+        banked = {}
 
         def add(c, b, eng, h0=0, h1=4):
             if h0 == 0:
-                sums[(c, b)] = epi.tile([P, 4, D], F32, tag="o", name="o_%d_%d" % (c, b))
+                sums[(c, b)] = epi.tile([P, 4, D], F32, tag="o", name="o_%d_%d" % (c, b), bufs=6)
             pairs = abt[(c, b)][:, h0:h1, :, :].rearrange("p h u (e j) -> p (h u) e j", e=2)
             eng.tensor_tensor(
                 out=sums[(c, b)][:, h0:h1, :].rearrange("p h (u j) -> p (h u) j", u=2),
@@ -293,7 +298,11 @@ def tile_multiheadattention_pa_kernel(
             pairs = abt[(c, b)][:].rearrange("p h u (e j) -> p (h u) e j", e=2)
             for e in range(2):
                 nc.tensor.matmul(out=bank[:], lhsT=ident[:], rhs=pairs[:, :, e, :], start=(e == 0), stop=(e == 1))
-            sums[(c, b)] = epi.tile([P, 4, D], F32, tag="o", name="o_%d_%d" % (c, b))
+            banked[(c, b)] = bank
+
+        def store_sum(c, b):
+            bank = banked[(c, b)]
+            sums[(c, b)] = epi.tile([P, 4, D], F32, tag="o", name="o_%d_%d" % (c, b), bufs=6)
             nc.scalar.copy(out=sums[(c, b)][:].rearrange("p h d -> p (h d)"), in_=bank[:])
             store(c, b, queue=nc.scalar)
 
@@ -311,7 +320,8 @@ def tile_multiheadattention_pa_kernel(
                 add_store(c, b, nc.gpsimd)
             products(c, 2, (0, 1, 2, 3))
             products(c, NB - 1, (0, 1, 2))
-            add_store(c, 2, nc.vector)
+            if c < NCH - 2:
+                add_store(c, 2, nc.vector)
             carried.append((c, NB - 1))
 
         def last_epilogue(c):
@@ -342,10 +352,14 @@ def tile_multiheadattention_pa_kernel(
                 turn(n, 0, range(4))
             if 2 <= c < NCH - 1:
                 turned_copy(c + 1, 0)
+            if c == NCH - 1:
+                sum_on_tensor(c - 1, 2)
             squares(c)
             if n < NCH:
                 widen(n, 1, (0,))
             norm(c, 1)
+            if c == NCH - 1:
+                store_sum(c - 1, 2)
             if n < NCH:
                 widen(n, 1, (1, 2, 3))
                 for g in (2, 3):
@@ -354,20 +368,24 @@ def tile_multiheadattention_pa_kernel(
             if n == 2:
                 turned_copy(n, 0)
 
-        widen_v(1, 0)
+        widen(1, 0, (0, 1))
+        widen_v(1, 0, (2, 3))
+        interleave(0, 0, 256, 512, nc.scalar.copy)
         widen(1, 1)
+        interleave(0, 0, 0, 256)
         interleave(1, 0)
         x_turn(0)
-        interleave(0, 0)
-        quantize(1, 0)
-        widen(1, 2)
-        interleave(0, 1)
         quantize(0, 0)
+        quantize(1, 0)
+        interleave(0, 1)
         x_turn(1)
-        x_quant(0)
+        interleave(1, 1)
         quantize(0, 1)
-        interleave(0, 2)
+        x_quant(0)
+        quantize(1, 1)
         x_quant(1)
+        widen(1, 2)
+        interleave(0, 2)
         x_turn(2)
         interleave(0, 3)
         quantize(0, 2)
@@ -376,13 +394,11 @@ def tile_multiheadattention_pa_kernel(
         spread_gains()
         widen(1, 3)
         quantize(0, 3)
-        interleave(1, 1)
+        interleave(1, 2)
         x_quant(3)
         tables()
-        interleave(1, 2)
-        quantize(1, 1)
-        interleave(1, 3)
         quantize(1, 2)
+        interleave(1, 3)
         quantize(1, 3)
         stage(0, range(NB))
         stage(1, range(NB))

@@ -59,11 +59,10 @@ def tile_multiheadattention_pa_kernel(
 
         wq_v = wq_bytes.rearrange("(g p t) n -> g p t n", p=P, t=4)
         wk_v = wk.rearrange("(g p t) n -> g p t n", p=P, t=4)
-        xin = [keep.tile([P, C], BF16, name="xin%d" % b) for b in range(NB)]
-        wkin = [None] + [keep.tile([P, 4, 512], BF16, name="wkin%d" % g) for g in range(1, PASSES)]
-        wkin0 = [keep.tile([P, 4, 256], BF16, name="wkin0_%d" % hf) for hf in range(2)]
+        xin = [keep.tile([P, C], BF16, name="xin%d" % b, align_bytes=256) for b in range(NB)]
+        wkin = [keep.tile([P, 4, 512], BF16, name="wkin%d" % g, align_bytes=256) for g in range(PASSES)]
         wqb = [
-            [keep.tile([P, 4, 512], U8, name="wqb%d_%d" % (j, g)) for g in range(PASSES)]
+            [keep.tile([P, 4, 512], U8, name="wqb%d_%d" % (j, g), align_bytes=256) for g in range(PASSES)]
             for j in range(4)
         ]
 
@@ -78,9 +77,7 @@ def tile_multiheadattention_pa_kernel(
 
         for hf in range(2):
             nc.sync.dma_start(out=wqb[0][0][:, 2 * hf : 2 * hf + 2, :], in_=wq_v[0][:, 2 * hf : 2 * hf + 2, 0:512])
-        for hf in range(2):
-            n0 = 256 * hf
-            nc.sync.dma_start(out=wkin0[hf][:], in_=wk_v[0][:, :, n0 : n0 + 256])
+        load_wk(0)
         load_wq(0, 1)
         load_x(0)
         load_wk(1)
@@ -88,8 +85,8 @@ def tile_multiheadattention_pa_kernel(
         load_wq(0, 2)
         load_wk(2)
         load_x(2)
-        load_wk(3)
         load_x(3)
+        load_wk(3)
         load_wq(0, 3)
         nc.sync.dma_start(out=grow[0:1, 0:D], in_=q_norm_w.unsqueeze(0))
         nc.sync.dma_start(out=grow[0:1, D : 2 * D], in_=k_norm_w.unsqueeze(0))
@@ -182,7 +179,7 @@ def tile_multiheadattention_pa_kernel(
                 )
 
         def interleave(c, g, n0=0, n1=512, copy=nc.vector.tensor_copy):
-            src = wkin0[n0 // 256][:] if (c, g) == (0, 0) else (wkin[g] if c == 0 else w16[(c, g)])[:, :, n0:n1]
+            src = (wkin[g] if c == 0 else w16[(c, g)])[:, :, n0:n1]
             if (c, g) not in wg:
                 wg[(c, g)] = wgp.tile([P, 2048], BF16, tag="wg", name="wg_%d_%d" % (c, g), align_bytes=64)
             copy(

@@ -19,7 +19,7 @@ P = 128
 PASSES = C // 512
 NCH = 5
 ORDER = 2 * [(0, 1, 2, 3)] + 3 * [(1, 2, 0, 3)]
-V_WIDENS = ((1, 0), (2, 3), (3, 3))
+S_PLANES = {2: (), 3: (0, 1)}
 FLOPS = 2 * NB * T * C * (H + KH) * D
 RUN = 8
 
@@ -359,9 +359,8 @@ def tile_multiheadattention_pa_kernel(
                 store_sum(c - 1, 2)
             if n < NCH:
                 widen(n, 1, (1, 2, 3))
-                for g in (2, 3):
-                    if (n, g) not in V_WIDENS:
-                        widen(n, g)
+                widen(n, 2)
+                widen(n, 3, S_PLANES.get(n, range(4)))
             if n == 2:
                 turned_copy(n, 0)
 
@@ -369,11 +368,11 @@ def tile_multiheadattention_pa_kernel(
         widen_v(1, 0, (2, 3))
         interleave(0, 0, 256, 512, nc.scalar.copy)
         widen(1, 1)
-        interleave(0, 0, 0, 256)
         interleave(1, 0)
+        interleave(0, 0, 0, 256)
         x_turn(0)
-        quantize(0, 0)
         quantize(1, 0)
+        quantize(0, 0)
         interleave(0, 1)
         x_turn(1)
         interleave(1, 1)
@@ -384,8 +383,8 @@ def tile_multiheadattention_pa_kernel(
         widen(1, 2)
         interleave(0, 2)
         x_turn(2)
-        interleave(0, 3)
         quantize(0, 2)
+        interleave(0, 3)
         x_quant(2)
         x_turn(3)
         spread_gains()
@@ -393,16 +392,15 @@ def tile_multiheadattention_pa_kernel(
         quantize(0, 3)
         interleave(1, 2)
         x_quant(3)
-        tables()
         quantize(1, 2)
         interleave(1, 3)
+        tables()
         quantize(1, 3)
         stage(0, range(NB))
         stage(1, range(NB))
         for c in range(2, NCH):
             staged = (0,) if c + 1 < NCH else (0, 1, 2)
-            if (c, 3) in V_WIDENS:
-                widen_v(c, 3)
+            widen_v(c, 3, [t for t in range(4) if t not in S_PLANES.get(c, range(4))])
             interleave(c, 1)
             interleave(c, 2)
             for i, g in enumerate(ORDER[c]):

from contextlib import ExitStack

import concourse.mybir as mybir
from concourse.masks import make_identity

F32 = mybir.dt.float32
BF16 = mybir.dt.bfloat16
U32 = mybir.dt.uint32
U8 = mybir.dt.uint8
FP8 = mybir.dt.float8_e4m3fn
FP8X4 = mybir.dt.float8_e4m3fn_x4
ACT = mybir.ActivationFunctionType
ALU = mybir.AluOpType

NB, T, C, H, KH, D = 4, 128, 2048, 16, 4, 128
HALF = D // 2
EPS = 1e-6
P = 128
PASSES = C // 512
NCH = 5
ORDER = 2 * [(0, 1, 2, 3)] + 3 * [(1, 2, 0, 3)]
S_PLANES = {2: (), 3: (0, 1)}
FLOPS = 2 * NB * T * C * (H + KH) * D
RUN = 8


def tile_multiheadattention_pa_kernel(
    tc, x, cos, sin, wq_bytes, wq_scale, wk, q_norm_w, k_norm_w, out_0, out_1
):
    nc = tc.nc
    with ExitStack() as ctx:
        const = ctx.enter_context(tc.tile_pool(name="const", bufs=1))
        keep = ctx.enter_context(tc.tile_pool(name="keep", bufs=1))
        w16p = ctx.enter_context(tc.tile_pool(name="w16p", bufs=5))
        wgp = ctx.enter_context(tc.tile_pool(name="wgp", bufs=4))
        epi = ctx.enter_context(tc.tile_pool(name="epi", bufs=4))
        small = ctx.enter_context(tc.tile_pool(name="small", bufs=8))
        psum = ctx.enter_context(tc.psum_pool(name="psum", bufs=6))
        ctx.enter_context(tc.manual_schedule())

        one1 = const.tile([P, 1], F32, name="one1")
        nc.vector.memset(one1[:], 1.0)
        warm = const.tile([P, 1], F32, name="warm")
        nc.scalar.activation(out=warm[:], in_=one1[:], func=ACT.Abs_reciprocal_sqrt)
        ident = const.tile([P, P], F32, name="ident")
        make_identity(nc, ident[:])
        ident16 = const.tile([P, P], BF16, name="ident16")
        nc.scalar.copy(out=ident16[:], in_=ident[:])
        sc = const.tile([P, 4 * PASSES], F32, name="sc")
        nc.sync.dma_start(
            out=sc[:].rearrange("p (g t) -> p g t", t=4),
            in_=wq_scale.rearrange("(g p t) o -> p g (t o)", p=P, t=4),
        )
        grow = const.tile([P, 2 * D], BF16, name="grow")
        nc.vector.memset(grow[:].bitcast(F32), 0.0)
        cs = const.tile([P, 2 * HALF], BF16, name="cs")
        ones = const.tile([P, P], BF16, name="ones")
        nc.vector.memset(ones[:], 1.0)

        wq_v = wq_bytes.rearrange("(g p t) n -> g p t n", p=P, t=4)
        wk_v = wk.rearrange("(g p t) n -> g p t n", p=P, t=4)
        xin = [keep.tile([P, C], BF16, name="xin%d" % b, align_bytes=256) for b in range(NB)]
        wkin = [keep.tile([P, 4, 512], BF16, name="wkin%d" % g, align_bytes=256) for g in range(PASSES)]
        wqb = [
            [keep.tile([P, 4, 512], U8, name="wqb%d_%d" % (j, g), align_bytes=256) for g in range(PASSES)]
            for j in range(4)
        ]

        def load_wq(j, g):
            nc.sync.dma_start(out=wqb[j][g][:], in_=wq_v[g][:, :, 512 * j : 512 * (j + 1)])

        def load_wk(g):
            nc.sync.dma_start(out=wkin[g][:], in_=wk_v[g])

        def load_x(b):
            nc.sync.dma_start(out=xin[b][:], in_=x[b])

        for hf in range(2):
            nc.sync.dma_start(out=wqb[0][0][:, 2 * hf : 2 * hf + 2, :], in_=wq_v[0][:, 2 * hf : 2 * hf + 2, 0:512])
        load_wk(0)
        load_wq(0, 1)
        load_x(0)
        load_wk(1)
        load_x(1)
        load_wq(0, 2)
        load_wk(2)
        load_x(2)
        load_x(3)
        load_wk(3)
        load_wq(0, 3)
        nc.sync.dma_start(out=grow[0:1, 0:D], in_=q_norm_w.unsqueeze(0))
        nc.sync.dma_start(out=grow[0:1, D : 2 * D], in_=k_norm_w.unsqueeze(0))
        nc.sync.dma_start(out=cs[:, 0:HALF], in_=cos.rearrange("o t u d -> (o t) (u d)"))
        nc.sync.dma_start(out=cs[:, HALF : 2 * HALF], in_=sin.rearrange("o t u d -> (o t) (u d)"))
        for j in range(1, 4):
            for g in range(PASSES):
                load_wq(j, g)

        tabq = const.tile([P, 2 * D], F32, name="tabq")
        tabk = const.tile([P, 2 * D], F32, name="tabk")

        gains = []

        def spread_gains():
            gps = psum.tile([P, 512], F32, tag="bank", name="gps", bufs=6)
            nc.tensor.matmul(out=gps[:, 0 : 2 * D], lhsT=ones[:], rhs=grow[:], start=True, stop=True)
            gains.append(gps)

        def tables():
            gps = gains[0]
            for i, tab in enumerate((tabq, tabk)):
                g1 = gps[:, i * D : i * D + HALF]
                g2 = gps[:, i * D + HALF : (i + 1) * D]
                cc = cs[:, 0:HALF]
                ssn = cs[:, HALF : 2 * HALF]
                nc.vector.tensor_tensor(out=tab[:, 0:HALF], in0=g1, in1=cc, op=ALU.mult)
                nc.vector.scalar_tensor_tensor(
                    out=tab[:, HALF:D], in0=g2, scalar=-1.0, in1=ssn, op0=ALU.mult, op1=ALU.mult
                )
                nc.vector.tensor_tensor(out=tab[:, D : D + HALF], in0=g1, in1=ssn, op=ALU.mult)
                nc.vector.tensor_tensor(out=tab[:, D + HALF : 2 * D], in0=g2, in1=cc, op=ALU.mult)

        xc = [keep.tile([P, 512], U32, name="xc%d" % b, align_bytes=64) for b in range(NB)]
        xs = [keep.tile([P, 512], U8, name="xs%d" % b, align_bytes=64) for b in range(NB)]
        xg = [keep.tile([P, C], BF16, name="xg%d" % b, align_bytes=64) for b in range(NB)]
        wc = [keep.tile([P, PASSES * 512], U32, name="wc%d" % c, align_bytes=64) for c in range(NCH)]
        ws = [keep.tile([P, PASSES * 512], U8, name="ws%d" % c, align_bytes=64) for c in range(NCH)]
        w16 = {}
        turned = {}
        wg = {}
        acc = {}
        rr = {}
        ssq = {}
        abt = {}

        def x_turn(b):
            words = xin[b][:].bitcast(F32)
            xgw = xg[b][:].bitcast(F32)
            for hf in range(2):
                bank = psum.tile([P, 512], F32, tag="bank", name="xt%d_%d" % (b, hf), bufs=6)
                for gi in range(2):
                    g = 2 * hf + gi
                    for u in range(2):
                        nc.tensor.transpose(
                            bank[:, (2 * gi + u) * P : (2 * gi + u + 1) * P],
                            words[:, 256 * g + u : 256 * (g + 1) : 2],
                            ident[:],
                        )
                nc.scalar.copy(
                    out=xgw[:, 512 * hf : 512 * (hf + 1)].rearrange("p (g r u) -> p g r u", g=2, u=2),
                    in_=bank[:].rearrange("p (g u r) -> p g r u", g=2, u=2),
                )

        def x_quant(b):
            nc.vector.quantize_mx(out=xc[b][:].bitcast(FP8X4), scales=xs[b][:], in_=xg[b][:])

        def w16_tile(c, g, tag, bufs):
            if (c, g) not in w16:
                w16[(c, g)] = w16p.tile([P, 4, 512], BF16, tag=tag, name="w16_%d_%d" % (c, g), bufs=bufs)
            return w16[(c, g)]

        def widen(c, g, planes=range(4)):
            for t in planes:
                nc.scalar.activation(
                    out=w16_tile(c, g, "w16", 5)[:, t, :],
                    in_=wqb[c - 1][g][:, t, :].bitcast(FP8),
                    func=ACT.Copy,
                    scale=sc[:, 4 * g + t : 4 * g + t + 1],
                )

        def widen_v(c, g, planes=range(4)):
            for t in planes:
                nc.vector.tensor_scalar(
                    out=w16_tile(c, g, "w16v", 2)[:, t, :],
                    in0=wqb[c - 1][g][:, t, :].bitcast(FP8),
                    scalar1=sc[:, 4 * g + t : 4 * g + t + 1],
                    scalar2=None,
                    op0=ALU.mult,
                )

        def interleave(c, g, n0=0, n1=512, copy=nc.vector.tensor_copy):
            src = (wkin[g] if c == 0 else w16[(c, g)])[:, :, n0:n1]
            if (c, g) not in wg:
                wg[(c, g)] = wgp.tile([P, 2048], BF16, tag="wg", name="wg_%d_%d" % (c, g), align_bytes=64)
            copy(
                out=wg[(c, g)][:, 4 * n0 : 4 * n1].rearrange("p (c i t) -> p c t i", i=RUN, t=4),
                in_=src.rearrange("p t (c i) -> p c t i", i=RUN),
            )

        def turn(c, g, quarters):
            for q in quarters:
                if q % 2 == 0:
                    turned[(c, g, q // 2)] = psum.tile([P, 1024], BF16, tag="turn", name="turn%d_%d_%d" % (c, g, q), bufs=2)
                nc.tensor.matmul(
                    out=turned[(c, g, q // 2)][:, 512 * (q % 2) : 512 * (q % 2 + 1)],
                    lhsT=ident16[:],
                    rhs=w16[(c, g)][:, :, P * q : P * (q + 1)].rearrange("p t n -> p n t"),
                    start=True,
                    stop=True,
                )

        def turned_copy(c, g):
            tg = wgp.tile([P, 2048], BF16, tag="wgt", name="wgt_%d_%d" % (c, g), align_bytes=64, bufs=2)
            for hf in range(2):
                nc.scalar.copy(out=tg[:, 1024 * hf : 1024 * (hf + 1)], in_=turned[(c, g, hf)][:])
            wg[(c, g)] = tg

        def quantize(c, g):
            cols = slice(512 * g, 512 * (g + 1))
            nc.vector.quantize_mx(out=wc[c][:, cols].bitcast(FP8X4), scales=ws[c][:, cols], in_=wg[(c, g)][:])

        def matmul(c, g, b):
            if g == ORDER[c][0]:
                last = c == NCH - 1 and b in (1, 2)
                acc[(c, b)] = psum.tile(
                    [P, 512], F32, tag="turn" if last else "bank", name="acc%d_%d" % (c, b), bufs=2 if last else 6
                )
            cols = slice(512 * g, 512 * (g + 1))
            nc.tensor.matmul_mx(
                out=acc[(c, b)][:],
                lhsT=xc[b][:, P * g : P * (g + 1)].bitcast(FP8X4),
                lhsT_scale=xs[b][:, P * g : P * (g + 1)],
                rhs=wc[c][:, cols].bitcast(FP8X4),
                rhs_scale=ws[c][:, cols],
                start=(g == ORDER[c][0]),
                stop=(g == ORDER[c][-1]),
            )

        def norm(c, half):
            r = small.tile([P, 8], F32, tag="r", name="r_%d_%d" % (c, half))
            nc.scalar.activation(
                out=r[:], in_=ssq[(c, half)][:], func=ACT.Abs_reciprocal_sqrt, scale=1.0 / D, bias=EPS
            )
            for i in range(2):
                rr[(c, 2 * half + i)] = r[:, 4 * i : 4 * i + 4]

        def squares(c):
            for i in range(16):
                b, h = i // 4, i % 4
                if i % 8 == 0:
                    ssq[(c, i // 8)] = small.tile([P, 8], F32, tag="ss", name="ss_%d_%d" % (c, i // 8))
                junk = small.tile([P, D], BF16, tag="junk", name="junk_%d_%d" % (c, i))
                nc.scalar.activation(
                    out=junk[:],
                    in_=acc[(c, b)][:, h * D : (h + 1) * D],
                    func=ACT.Square,
                    accum_out=ssq[(c, i // 8)][:, i % 8 : i % 8 + 1],
                )
                if i == 8:
                    norm(c, 0)

        def products(c, b, heads):
            a = acc[(c, b)]
            tab = tabk if c == 0 else tabq
            if heads[0] == 0:
                abt[(c, b)] = epi.tile([P, 4, 2, D], F32, tag="ab", name="ab_%d_%d" % (c, b))
            ab = abt[(c, b)]
            for h in heads:
                nc.vector.scalar_tensor_tensor(
                    out=ab[:, h, :, :],
                    in0=a[:, h * D : (h + 1) * D].unsqueeze(1).to_broadcast([P, 2, D]),
                    scalar=rr[(c, b)][:, h : h + 1],
                    in1=tab[:].rearrange("p (u d) -> p u d", u=2),
                    op0=ALU.mult,
                    op1=ALU.mult,
                )

        sums = {}
        banked = {}

        def add(c, b, eng, h0=0, h1=4):
            if h0 == 0:
                sums[(c, b)] = epi.tile([P, 4, D], F32, tag="o", name="o_%d_%d" % (c, b), bufs=6)
            pairs = abt[(c, b)][:, h0:h1, :, :].rearrange("p h u (e j) -> p (h u) e j", e=2)
            eng.tensor_tensor(
                out=sums[(c, b)][:, h0:h1, :].rearrange("p h (u j) -> p (h u) j", u=2),
                in0=pairs[:, :, 0, :],
                in1=pairs[:, :, 1, :],
                op=ALU.add,
            )

        def store(c, b, h0=0, h1=4, queue=nc.sync):
            src = sums[(c, b)][:, h0:h1, :]
            if c == 0:
                queue.dma_start(out=out_1[b][:, h0:h1, :], in_=src)
            else:
                queue.dma_start(out=out_0[b][:, 4 * (c - 1) + h0 : 4 * (c - 1) + h1, :], in_=src)

        def add_store(c, b, eng):
            add(c, b, eng)
            store(c, b)

        def sum_on_tensor(c, b):
            bank = psum.tile([P, 512], F32, tag="bank", name="sum_%d_%d" % (c, b), bufs=6)
            pairs = abt[(c, b)][:].rearrange("p h u (e j) -> p (h u) e j", e=2)
            for e in range(2):
                nc.tensor.matmul(out=bank[:], lhsT=ident[:], rhs=pairs[:, :, e, :], start=(e == 0), stop=(e == 1))
            banked[(c, b)] = bank

        def store_sum(c, b):
            bank = banked[(c, b)]
            sums[(c, b)] = epi.tile([P, 4, D], F32, tag="o", name="o_%d_%d" % (c, b), bufs=6)
            nc.scalar.copy(out=sums[(c, b)][:].rearrange("p h d -> p (h d)"), in_=bank[:])
            store(c, b, queue=nc.scalar)

        carried = []

        def finish_carried():
            for c, b in carried:
                products(c, b, (3,))
                add_store(c, b, nc.gpsimd)
            carried.clear()

        def epilogue(c):
            for b in range(2):
                products(c, b, (0, 1, 2, 3))
                add_store(c, b, nc.gpsimd)
            products(c, 2, (0, 1, 2, 3))
            products(c, NB - 1, (0, 1, 2))
            if c < NCH - 2:
                add_store(c, 2, nc.vector)
            carried.append((c, NB - 1))

        def last_epilogue(c):
            for b in range(2):
                products(c, b, (0, 1, 2, 3))
                add_store(c, b, nc.gpsimd)
            products(c, 2, (0, 1, 2, 3))
            products(c, 3, (0, 1, 2, 3))
            add_store(c, 2, nc.vector)
            for h in (0, 2):
                add(c, 3, nc.vector, h, h + 2)
                store(c, 3, h, h + 2)

        def passes(c, banks):
            for b in banks:
                for g in ORDER[c]:
                    matmul(c, g, b)

        def stage(c, late):
            n = c + 2
            finish_carried()
            if c > 0:
                epilogue(c - 1)
            if n < NCH:
                widen(n, 0)
            passes(c, late)
            if n == 2:
                turn(n, 0, range(4))
            if 2 <= c < NCH - 1:
                turned_copy(c + 1, 0)
            if c == NCH - 1:
                sum_on_tensor(c - 1, 2)
            squares(c)
            if n < NCH:
                widen(n, 1, (0,))
            norm(c, 1)
            if c == NCH - 1:
                store_sum(c - 1, 2)
            if n < NCH:
                widen(n, 1, (1, 2, 3))
                widen(n, 2)
                widen(n, 3, S_PLANES.get(n, range(4)))
            if n == 2:
                turned_copy(n, 0)

        widen(1, 0, (0, 1))
        widen_v(1, 0, (2, 3))
        interleave(0, 0, 256, 512, nc.scalar.copy)
        widen(1, 1)
        interleave(1, 0)
        interleave(0, 0, 0, 256)
        x_turn(0)
        quantize(1, 0)
        quantize(0, 0)
        interleave(0, 1)
        x_turn(1)
        interleave(1, 1)
        quantize(0, 1)
        x_quant(0)
        quantize(1, 1)
        x_quant(1)
        widen(1, 2)
        interleave(0, 2)
        x_turn(2)
        quantize(0, 2)
        interleave(0, 3)
        x_quant(2)
        x_turn(3)
        spread_gains()
        widen(1, 3)
        quantize(0, 3)
        interleave(1, 2)
        x_quant(3)
        quantize(1, 2)
        interleave(1, 3)
        tables()
        quantize(1, 3)
        stage(0, range(NB))
        stage(1, range(NB))
        for c in range(2, NCH):
            staged = (0,) if c + 1 < NCH else (0, 1, 2)
            widen_v(c, 3, [t for t in range(4) if t not in S_PLANES.get(c, range(4))])
            interleave(c, 1)
            interleave(c, 2)
            for i, g in enumerate(ORDER[c]):
                quantize(c, g)
                for b in staged:
                    matmul(c, g, b)
                if c + 1 < NCH:
                    turn(c + 1, 0, (i,))
                if i == 0:
                    interleave(c, 3)
            stage(c, [b for b in range(NB) if b not in staged])
        finish_carried()
        last_epilogue(NCH - 1)
